import numpy as np
import ml_dtypes


def mxq(x, axis, fmt="e4m3"):
    dtype, down = {"e4m3": (ml_dtypes.float8_e4m3fn, 7), "e5m2": (ml_dtypes.float8_e5m2, 14)}[fmt]
    v = np.moveaxis(np.asarray(x, np.float32).astype(ml_dtypes.bfloat16).astype(np.float64), axis, -1)
    blocks = v.reshape(v.shape[:-1] + (-1, 32))
    amax = np.abs(blocks).max(-1, keepdims=True)
    byte = np.maximum(np.where(amax > 0, np.frexp(amax)[1] - 1 + 127, 0) - down, 1)
    scale = np.exp2(byte - 127.0)
    codes = (blocks / scale).astype(np.float32).astype(dtype).astype(np.float64)
    return np.moveaxis((codes * scale).reshape(v.shape), -1, axis)


WIDE = False


def mx_kscale(k):
    if not WIDE:
        return np.ones(k)
    levels = np.array([10, -10, 5, -5, 0])
    if k % 512:
        return np.exp2(np.random.permutation(np.resize(levels, k // 32))).repeat(32)
    a = np.empty((k // 512, 16))
    for p in range(k // 512):
        a[p, :8] = np.random.permutation(np.resize(levels, 8))
        for g in range(8):
            far = levels[np.abs(levels - a[p, g]) >= 10]
            a[p, g + 8] = far[np.random.randint(len(far))]
    return np.exp2(a.ravel()).repeat(32)


BF16 = ml_dtypes.bfloat16


def bf(x):
    return np.asarray(x, np.float32).astype(BF16)


def f64(x):
    return np.asarray(x).astype(np.float64)


B, DD, DK, CI, CO, L, NLC, PAD, KL = 1, 2, 2, 512, 128, 256, 4, 4, 9


def seg_lengths():
    cover = (L + PAD + PAD) // NLC - PAD - PAD
    lens = [cover] * NLC
    lens[-1] = L - cover * (NLC - 1)
    return lens


def draw0():
    s = mx_kscale(CI)
    x = np.random.standard_normal((B, DD, DK, CI, L)) * s[:, None]
    weight = np.random.standard_normal((DD, DK, CO, CI, NLC, KL)) / np.sqrt(CI * KL) / s[:, None, None]
    bias = np.random.standard_normal((DD, DK, CO, NLC)) * 0.5
    return {"x": bf(x), "weight": bf(weight[..., None, :]), "conv_bias_param": bf(bias[..., None])}


def core(x, weight, conv_bias_param):
    xq = mxq(f64(x), 3, "e4m3")
    wq = mxq(f64(weight), 3, "e4m3")
    bias = f64(conv_bias_param)
    outs, start = [], 0
    for i, ln in enumerate(seg_lengths()):
        acc = np.zeros((B, DD, DK, CO, ln))
        for f in range(KL):
            lo = max(start, PAD - f)
            hi = min(start + ln, L + PAD - f)
            xs = xq[..., lo + f - PAD:hi + f - PAD].swapaxes(-1, -2)
            wf = wq[:, :, :, :, i, 0, f].swapaxes(-1, -2)
            acc[..., lo - start:hi - start] += (xs @ wf).swapaxes(-1, -2)
        outs.append(acc + bias[None, :, :, :, i, :])
        start += ln
    return np.concatenate(outs, axis=-1)


def e4m3fn_bytes(y):
    return np.clip(np.asarray(y, np.float64), -448.0, 448.0).astype(np.float32).astype(ml_dtypes.float8_e4m3fn).view(np.uint8)


def e4m3fn_values(b):
    return np.asarray(b, np.uint8).view(ml_dtypes.float8_e4m3fn).astype(np.float64)


def setup_inputs():
    d = draw0()
    x0 = np.asarray(d['weight']).astype(np.float64)
    s = (np.max(np.abs(x0), axis=(0, 1, 2, 4, 5, 6), keepdims=True) / 448.0).astype(np.float32)
    out = {}
    for k, v in d.items():
        if k == 'weight':
            out['weight_bytes'] = e4m3fn_bytes(x0 / s.astype(np.float64))
            out['weight_scale'] = s
        else:
            out[k] = v
    return out


def reference(x, weight_bytes, weight_scale, conv_bias_param):
    return core(x, e4m3fn_values(weight_bytes) * weight_scale.astype(np.float64), conv_bias_param)

@@ -1,0 +1,226 @@
+from contextlib import ExitStack
+
+import concourse.mybir as mybir
+from concourse.masks import make_identity
+
+F32 = mybir.dt.float32
+BF16 = mybir.dt.bfloat16
+I32 = mybir.dt.int32
+U32 = mybir.dt.uint32
+U8 = mybir.dt.uint8
+FP8 = mybir.dt.float8_e4m3fn
+FP8X4 = mybir.dt.float8_e4m3fn_x4
+MULT = mybir.AluOpType.mult
+IDENT = mybir.ActivationFunctionType.Identity
+
+P = 128
+NDK = 4
+CI = 512
+CO = 128
+L = 256
+NSEG = 4
+KL = 9
+PAD = 4
+NS = NSEG * KL
+ROW = CI * NS
+CHUNK = 3072
+NCH = ROW // CHUNK
+NBANK = NS // 2
+WSTEP = 4 * NS // 2
+SEG_START = (0, 58, 116, 174)
+SEG_LEN = (58, 58, 58, 82)
+SEG_WIN = (0, 0, 64, 128)
+GROUPS = ((0, 4), (4, 4), (8, 4), (12, 4), (16, 2))
+LOOKAHEAD = 5
+
+FLOPS = 2 * NDK * CO * CI * KL * L
+
+
+def tile_partiallyunsharedconv1d_pa_kernel(tc, x, weight_bytes, weight_scale, conv_bias_param, out):
+    nc = tc.nc
+    with ExitStack() as ctx:
+        const = ctx.enter_context(tc.tile_pool(name="const", bufs=1))
+        wb_pool = ctx.enter_context(tc.tile_pool(name="wb_pool", bufs=NCH))
+        wbf_pool = ctx.enter_context(tc.tile_pool(name="wbf_pool", bufs=2))
+        grp_pool = ctx.enter_context(tc.tile_pool(name="grp_pool", bufs=3))
+        wq_pool = ctx.enter_context(tc.tile_pool(name="wq_pool", bufs=2))
+        out_pool = ctx.enter_context(tc.tile_pool(name="out_pool", bufs=2))
+        ps_pool = ctx.enter_context(tc.psum_pool(name="ps_pool", bufs=6))
+        acc_pool = ctx.enter_context(tc.psum_pool(name="acc_pool", bufs=2))
+
+        w_rows = weight_bytes.rearrange("d k o i g u f -> (d k) o (i g u f)")
+        out_rows = out.rearrange("b d k o l -> (b d k) o l")
+
+        state = {}
+
+        def load_w(dk, c):
+            wbytes = wb_pool.tile([P, CHUNK], U8, name="wbytes")
+            nc.sync.dma_start(out=wbytes[:], in_=w_rows[dk][:, c * CHUNK:(c + 1) * CHUNK])
+            state[("wbytes", dk, c)] = wbytes
+
+        def cast_w(dk, c, on_vector):
+            if c == 0:
+                state[("wbf", dk)] = wbf_pool.tile([P, ROW], BF16, name="wbf")
+            wbf = state[("wbf", dk)]
+            src = state[("wbytes", dk, c)][:].bitcast(FP8)
+            dst = wbf[:, c * CHUNK:(c + 1) * CHUNK]
+            if on_vector:
+                nc.vector.tensor_copy(out=dst, in_=src)
+            else:
+                nc.scalar.copy(out=dst, in_=src)
+
+        zero = const.tile([P, 1], F32, name="zero")
+        nc.vector.memset(zero[:], 0.0)
+        warm = const.tile([P, 1], F32, name="warm")
+        nc.scalar.activation(out=warm[:], in_=zero[:], func=IDENT, bias=zero[:, 0:1])
+        xraw = const.tile([P, NDK * 4 * L], BF16, name="xraw")
+        nc.sync.dma_start(
+            out=xraw[:].rearrange("p (d n) -> p d n", d=NDK),
+            in_=x.rearrange("b d k (p t) l -> p (b d k) (t l)", t=4),
+        )
+        for c in range(NCH):
+            load_w(0, c)
+
+        sc = const.tile([P, 1, 1, 4], F32, name="sc")
+        nc.scalar.dma_start(
+            out=sc[:].rearrange("p a b t -> p (a b t)"),
+            in_=weight_scale.rearrange("a b c i e f g -> (a b c i e f g)").rearrange("(p t) -> p t", t=4),
+        )
+        bias_bf = const.tile([P, NDK * NSEG], BF16, name="bias_bf")
+        nc.scalar.dma_start(
+            out=bias_bf[:].rearrange("p (a g) -> p a g", a=NDK),
+            in_=conv_bias_param.rearrange("d k o g u -> o (d k) (g u)"),
+        )
+        ident = const.tile([P, P], F32, name="ident")
+        make_identity(nc, ident[:])
+
+        xc = const.tile([P, KL * NDK * L], U32, name="xc", align_bytes=64)
+        xs = const.tile([P, KL * NDK * L], U8, name="xs", align_bytes=64)
+        xg = const.tile([P, NDK * L * 4], BF16, name="xg", align_bytes=64)
+        nc.vector.memset(xs[:].bitcast(I32), 0)
+        xc_rows = xc[:].rearrange("p (g c) -> p g c", c=L)
+        nc.vector.memset(xc_rows[:, :, 0:PAD].bitcast(I32), 0)
+        nc.vector.memset(xc_rows[:, :, L - PAD:L].bitcast(I32), 0)
+        bias = const.tile([P, NDK * NSEG], F32, name="bias")
+        nc.vector.tensor_copy(out=bias[:], in_=bias_bf[:])
+
+        nc.vector.tensor_copy(
+            out=xg[:].rearrange("p (d l t) -> p d l t", d=NDK, t=4),
+            in_=xraw[:].rearrange("p (d t l) -> p d l t", d=NDK, t=4),
+        )
+        mid = PAD * NDK * L
+        nc.vector.quantize_mx(
+            out=xc[:, mid:mid + NDK * L].bitcast(FP8X4),
+            scales=xs[:, mid:mid + NDK * L],
+            in_=xg[:],
+        )
+        xc4 = xc[:].rearrange("p (f d c) -> p f d c", f=KL, d=NDK)
+        xs4 = xs[:].rearrange("p (f d c) -> p f d c", f=KL, d=NDK)
+        for f in range(KL):
+            sh = f - PAD
+            if sh == 0:
+                continue
+            lo, hi = max(0, -sh), L - max(0, sh)
+            nc.vector.tensor_copy(
+                out=xc4[:, f, :, lo:hi].bitcast(I32), in_=xc4[:, PAD, :, lo + sh:hi + sh].bitcast(I32)
+            )
+            nc.vector.tensor_copy(out=xs4[:, f, :, lo:hi], in_=xs4[:, PAD, :, lo + sh:hi + sh])
+
+        for c in range(NCH):
+            cast_w(0, c, on_vector=(c == NCH - 1))
+            load_w(1, c)
+
+        def transposes(b):
+            dk, s2 = divmod(b, NBANK)
+            words = state[("wbf", dk)][:].bitcast(F32)
+            ps = ps_pool.tile([P, 4 * P], F32, name="ps")
+            for t in range(4):
+                nc.tensor.transpose(
+                    ps[:, t * P:(t + 1) * P], words[:, t * (NS // 2) + s2:ROW // 2:WSTEP], ident[:]
+                )
+            state[("ps", b)] = ps
+
+        def scale_bank(b):
+            dk, s2 = divmod(b, NBANK)
+            for g, (first, n) in enumerate(GROUPS):
+                if first <= s2 < first + n:
+                    if s2 == first:
+                        state[("grp", dk, g)] = grp_pool.tile([P, 4096], BF16, name="grp", align_bytes=64)
+                    grp = state[("grp", dk, g)]
+                    j = s2 - first
+                    nc.vector.tensor_tensor(
+                        out=grp[:, j * 1024:(j + 1) * 1024].rearrange("p (e o t) -> p e o t", e=2, t=4),
+                        in0=state[("ps", b)][:].bitcast(BF16).rearrange("p (t o e) -> p e o t", t=4, e=2),
+                        in1=sc[:].to_broadcast([P, 2, P, 4]),
+                        op=MULT,
+                    )
+                    return (dk, g) if j == n - 1 else None
+            return None
+
+        def quantise(dk, g):
+            first, n = GROUPS[g]
+            if g == 0:
+                state[("wc", dk)] = wq_pool.tile([P, NS * P], U32, name="wc", align_bytes=64)
+                state[("ws", dk)] = wq_pool.tile([P, NS * P], U8, name="ws", align_bytes=64)
+            a, w = first * 256, n * 256
+            nc.vector.quantize_mx(
+                out=state[("wc", dk)][:, a:a + w].bitcast(FP8X4),
+                scales=state[("ws", dk)][:, a:a + w],
+                in_=state[("grp", dk, g)][:, 0:4 * w],
+            )
+
+        def matmuls(dk, g):
+            first, n = GROUPS[g]
+            if g == 0:
+                state[("acc", dk)] = acc_pool.tile([P, NSEG * P], F32, name="acc")
+            acc = state[("acc", dk)]
+            wc, ws = state[("wc", dk)], state[("ws", dk)]
+            for s in range(2 * first, 2 * (first + n)):
+                seg, f = divmod(s, KL)
+                w0 = SEG_WIN[seg]
+                nc.tensor.matmul_mx(
+                    out=acc[:, seg * P:(seg + 1) * P],
+                    lhsT=wc[:, s * P:(s + 1) * P].bitcast(FP8X4),
+                    lhsT_scale=ws[:, s * P:(s + 1) * P],
+                    rhs=xc4[:, f, dk, w0:w0 + P].bitcast(FP8X4),
+                    rhs_scale=xs4[:, f, dk, w0:w0 + P],
+                    start=(f == 0),
+                    stop=(f == KL - 1),
+                )
+            if g == len(GROUPS) - 1:
+                osb = out_pool.tile([P, L], F32, name="osb")
+                for seg in range(NSEG):
+                    l0, ln = SEG_START[seg], SEG_LEN[seg]
+                    a0 = seg * P + l0 - SEG_WIN[seg]
+                    nc.scalar.activation(
+                        out=osb[:, l0:l0 + ln], in_=acc[:, a0:a0 + ln], func=IDENT,
+                        bias=bias[:, dk * NSEG + seg:dk * NSEG + seg + 1],
+                    )
+                nc.scalar.dma_start(out=out_rows[dk], in_=osb[:])
+
+        total = NDK * NBANK
+        for b in range(LOOKAHEAD):
+            transposes(b)
+        to_quantise = None
+        to_multiply = None
+        for b in range(total):
+            dk, s2 = divmod(b, NBANK)
+            if s2 % 2 == 0 and s2 // 2 < NCH and dk + 1 < NDK:
+                c = s2 // 2
+                cast_w(dk + 1, c, on_vector=False)
+                if dk + 2 < NDK:
+                    load_w(dk + 2, c)
+            if b + LOOKAHEAD < total:
+                transposes(b + LOOKAHEAD)
+            closed = scale_bank(b)
+            if to_multiply is not None:
+                matmuls(*to_multiply)
+                to_multiply = None
+            if to_quantise is not None:
+                quantise(*to_quantise)
+                to_multiply = to_quantise
+            to_quantise = closed
+        if to_multiply is not None:
+            matmuls(*to_multiply)
+        quantise(*to_quantise)
+        matmuls(*to_quantise)

@@ -11,6 +11,7 @@ U8 = mybir.dt.uint8
 FP8 = mybir.dt.float8_e4m3fn
 FP8X4 = mybir.dt.float8_e4m3fn_x4
 MULT = mybir.AluOpType.mult
+ADD = mybir.AluOpType.add
 IDENT = mybir.ActivationFunctionType.Identity
 
 P = 128
@@ -25,13 +26,19 @@ NS = NSEG * KL
 ROW = CI * NS
 CHUNK = 3072
 NCH = ROW // CHUNK
-NBANK = NS // 2
-WSTEP = 4 * NS // 2
+NUNIT = NS // 4
+NBANK = 2 * NUNIT
+HALF = NS // 2
+WSTEP = 4 * HALF
 SEG_START = (0, 58, 116, 174)
 SEG_LEN = (58, 58, 58, 82)
 SEG_WIN = (0, 0, 64, 128)
-GROUPS = ((0, 4), (4, 4), (8, 4), (12, 4), (16, 2))
+MARGIN = 64
+XROW = MARGIN + L
 LOOKAHEAD = 5
+SG_UNITS = ((8,), (8,), (6, 8), (0, 1, 3, 5, 7))
+SG_DUE = (5, 5, 5, 4)
+HEAD_ON_VECTOR = (3, 4, 5)
 
 FLOPS = 2 * NDK * CO * CI * KL * L
 
@@ -42,7 +49,8 @@ def tile_partiallyunsharedconv1d_pa_kernel(tc, x, weight_bytes, weight_scale, co
         const = ctx.enter_context(tc.tile_pool(name="const", bufs=1))
         wb_pool = ctx.enter_context(tc.tile_pool(name="wb_pool", bufs=NCH))
         wbf_pool = ctx.enter_context(tc.tile_pool(name="wbf_pool", bufs=2))
-        grp_pool = ctx.enter_context(tc.tile_pool(name="grp_pool", bufs=3))
+        grp_pool = ctx.enter_context(tc.tile_pool(name="grp_pool", bufs=5))
+        pl_pool = ctx.enter_context(tc.tile_pool(name="pl_pool", bufs=2))
         wq_pool = ctx.enter_context(tc.tile_pool(name="wq_pool", bufs=2))
         out_pool = ctx.enter_context(tc.tile_pool(name="out_pool", bufs=2))
         ps_pool = ctx.enter_context(tc.psum_pool(name="ps_pool", bufs=6))
@@ -59,7 +67,7 @@ def tile_partiallyunsharedconv1d_pa_kernel(tc, x, weight_bytes, weight_scale, co
             state[("wbytes", dk, c)] = wbytes
 
         def cast_w(dk, c, on_vector):
-            if c == 0:
+            if ("wbf", dk) not in state:
                 state[("wbf", dk)] = wbf_pool.tile([P, ROW], BF16, name="wbf")
             wbf = state[("wbf", dk)]
             src = state[("wbytes", dk, c)][:].bitcast(FP8)
@@ -74,11 +82,16 @@ def tile_partiallyunsharedconv1d_pa_kernel(tc, x, weight_bytes, weight_scale, co
         warm = const.tile([P, 1], F32, name="warm")
         nc.scalar.activation(out=warm[:], in_=zero[:], func=IDENT, bias=zero[:, 0:1])
         xraw = const.tile([P, NDK * 4 * L], BF16, name="xraw")
-        nc.sync.dma_start(
-            out=xraw[:].rearrange("p (d n) -> p d n", d=NDK),
-            in_=x.rearrange("b d k (p t) l -> p (b d k) (t l)", t=4),
-        )
-        for c in range(NCH):
+        x_rows = x.rearrange("b d k (p t) l -> (b d k) p (t l)", t=4)
+
+        def load_x(dk):
+            nc.sync.dma_start(out=xraw[:, dk * 4 * L:(dk + 1) * 4 * L], in_=x_rows[dk])
+
+        load_x(0)
+        load_w(0, 0)
+        for dk in range(1, NDK):
+            load_x(dk)
+        for c in range(1, NCH):
             load_w(0, c)
 
         sc = const.tile([P, 1, 1, 4], F32, name="sc")
@@ -95,87 +108,126 @@ def tile_partiallyunsharedconv1d_pa_kernel(tc, x, weight_bytes, weight_scale, co
         make_identity(nc, ident[:])
 
         xc = const.tile([P, KL * NDK * L], U32, name="xc", align_bytes=64)
-        xs = const.tile([P, KL * NDK * L], U8, name="xs", align_bytes=64)
+        xs = const.tile([P, KL * NDK * XROW], U8, name="xs", align_bytes=64)
         xg = const.tile([P, NDK * L * 4], BF16, name="xg", align_bytes=64)
         nc.vector.memset(xs[:].bitcast(I32), 0)
         xc_rows = xc[:].rearrange("p (g c) -> p g c", c=L)
         nc.vector.memset(xc_rows[:, :, 0:PAD].bitcast(I32), 0)
         nc.vector.memset(xc_rows[:, :, L - PAD:L].bitcast(I32), 0)
         bias = const.tile([P, NDK * NSEG], F32, name="bias")
-        nc.vector.tensor_copy(out=bias[:], in_=bias_bf[:])
 
-        nc.vector.tensor_copy(
-            out=xg[:].rearrange("p (d l t) -> p d l t", d=NDK, t=4),
-            in_=xraw[:].rearrange("p (d t l) -> p d l t", d=NDK, t=4),
-        )
-        mid = PAD * NDK * L
-        nc.vector.quantize_mx(
-            out=xc[:, mid:mid + NDK * L].bitcast(FP8X4),
-            scales=xs[:, mid:mid + NDK * L],
-            in_=xg[:],
-        )
         xc4 = xc[:].rearrange("p (f d c) -> p f d c", f=KL, d=NDK)
         xs4 = xs[:].rearrange("p (f d c) -> p f d c", f=KL, d=NDK)
+
+        def interleave_x(dk):
+            cols = slice(dk * 4 * L, (dk + 1) * 4 * L)
+            nc.vector.tensor_copy(
+                out=xg[:, cols].rearrange("p (l t) -> p l t", t=4), in_=xraw[:, cols].rearrange("p (t l) -> p l t", t=4)
+            )
+
+        def quantise_x(dk):
+            nc.vector.quantize_mx(
+                out=xc4[:, PAD, dk, :].bitcast(FP8X4),
+                scales=xs4[:, PAD, dk, MARGIN:XROW],
+                in_=xg[:, dk * 4 * L:(dk + 1) * 4 * L],
+            )
+
+        interleave_x(0)
+        for dk in range(1, NDK):
+            interleave_x(dk)
+            quantise_x(dk - 1)
+        nc.vector.tensor_copy(out=bias[:], in_=bias_bf[:])
+        quantise_x(NDK - 1)
+        for sh in (1, 2, 3):
+            nc.vector.tensor_copy(
+                out=xs4[:, PAD + sh, :, MARGIN - sh:XROW - sh], in_=xs4[:, PAD, :, MARGIN:XROW]
+            )
+        for f in (0, 1, 2, 3):
+            nc.sync.dma_start(
+                out=xs4[:, f, :, MARGIN:XROW].bitcast(I32), in_=xs4[:, f + PAD, :, MARGIN - 4:XROW - 4].bitcast(I32)
+            )
+        nc.sync.dma_start(
+            out=xs4[:, 2 * PAD, :, MARGIN:XROW - 4].bitcast(I32), in_=xs4[:, PAD, :, MARGIN + 4:XROW].bitcast(I32)
+        )
         for f in range(KL):
             sh = f - PAD
-            if sh == 0:
-                continue
-            lo, hi = max(0, -sh), L - max(0, sh)
-            nc.vector.tensor_copy(
-                out=xc4[:, f, :, lo:hi].bitcast(I32), in_=xc4[:, PAD, :, lo + sh:hi + sh].bitcast(I32)
-            )
-            nc.vector.tensor_copy(out=xs4[:, f, :, lo:hi], in_=xs4[:, PAD, :, lo + sh:hi + sh])
+            if sh != 0:
+                lo, hi = max(0, -sh), L - max(0, sh)
+                nc.sync.dma_start(
+                    out=xc4[:, f, :, lo:hi].bitcast(I32), in_=xc4[:, PAD, :, lo + sh:hi + sh].bitcast(I32)
+                )
 
         for c in range(NCH):
-            cast_w(0, c, on_vector=(c == NCH - 1))
+            cast_w(0, c, on_vector=(c in HEAD_ON_VECTOR))
             load_w(1, c)
 
+        banks = [(dk, u, h) for dk in range(NDK) for u in range(NUNIT) for h in range(2)]
+
         def transposes(b):
-            dk, s2 = divmod(b, NBANK)
+            dk, u, h = banks[b]
             words = state[("wbf", dk)][:].bitcast(F32)
             ps = ps_pool.tile([P, 4 * P], F32, name="ps")
-            for t in range(4):
-                nc.tensor.transpose(
-                    ps[:, t * P:(t + 1) * P], words[:, t * (NS // 2) + s2:ROW // 2:WSTEP], ident[:]
-                )
+            for q in range(4):
+                if u in SG_UNITS[dk]:
+                    t, s2 = 2 * h + q // 2, 2 * u + q % 2
+                else:
+                    t, s2 = q, 2 * u + h
+                nc.tensor.transpose(ps[:, q * P:(q + 1) * P], words[:, t * HALF + s2:ROW // 2:WSTEP], ident[:])
             state[("ps", b)] = ps
 
-        def scale_bank(b):
-            dk, s2 = divmod(b, NBANK)
-            for g, (first, n) in enumerate(GROUPS):
-                if first <= s2 < first + n:
-                    if s2 == first:
-                        state[("grp", dk, g)] = grp_pool.tile([P, 4096], BF16, name="grp", align_bytes=64)
-                    grp = state[("grp", dk, g)]
-                    j = s2 - first
-                    nc.vector.tensor_tensor(
+        def consume(b):
+            dk, u, h = banks[b]
+            ps = state[("ps", b)]
+            if h == 0:
+                state[("grp", dk, u)] = grp_pool.tile([P, 2048], BF16, name="grp", align_bytes=64)
+            grp = state[("grp", dk, u)]
+            if u not in SG_UNITS[dk]:
+                nc.vector.tensor_tensor(
+                    out=grp[:, h * 1024:(h + 1) * 1024].rearrange("p (e o t) -> p e o t", e=2, t=4),
+                    in0=ps[:].bitcast(BF16).rearrange("p (t o e) -> p e o t", t=4, e=2),
+                    in1=sc[:].to_broadcast([P, 2, P, 4]),
+                    op=MULT,
+                )
+                return True
+            if h == 0:
+                state[("planes", dk, u)] = pl_pool.tile([P, 2048], BF16, name="planes")
+            planes = state[("planes", dk, u)]
+            for q in range(2):
+                t = 2 * h + q
+                nc.scalar.activation(
+                    out=planes[:, t * 512:(t + 1) * 512], in_=ps[:, q * 256:(q + 1) * 256].bitcast(BF16),
+                    func=IDENT, scale=sc[:, 0, 0, t:t + 1],
+                )
+            if h == 1:
+                rows = planes[:].rearrange("p (t j o e) -> p j e o t", t=4, j=2, e=2)
+                for j in range(2):
+                    nc.gpsimd.tensor_scalar(
                         out=grp[:, j * 1024:(j + 1) * 1024].rearrange("p (e o t) -> p e o t", e=2, t=4),
-                        in0=state[("ps", b)][:].bitcast(BF16).rearrange("p (t o e) -> p e o t", t=4, e=2),
-                        in1=sc[:].to_broadcast([P, 2, P, 4]),
-                        op=MULT,
+                        in0=rows[:, j], scalar1=1.0, scalar2=0.0, op0=MULT, op1=ADD,
                     )
-                    return (dk, g) if j == n - 1 else None
-            return None
+            return False
 
-        def quantise(dk, g):
-            first, n = GROUPS[g]
-            if g == 0:
+        def quantise(dk, u):
+            if ("wc", dk) not in state:
                 state[("wc", dk)] = wq_pool.tile([P, NS * P], U32, name="wc", align_bytes=64)
                 state[("ws", dk)] = wq_pool.tile([P, NS * P], U8, name="ws", align_bytes=64)
-            a, w = first * 256, n * 256
+                state[("next_s", dk)] = 0
             nc.vector.quantize_mx(
-                out=state[("wc", dk)][:, a:a + w].bitcast(FP8X4),
-                scales=state[("ws", dk)][:, a:a + w],
-                in_=state[("grp", dk, g)][:, 0:4 * w],
+                out=state[("wc", dk)][:, u * 512:(u + 1) * 512].bitcast(FP8X4),
+                scales=state[("ws", dk)][:, u * 512:(u + 1) * 512],
+                in_=state[("grp", dk, u)][:],
             )
+            state[("done", dk, u)] = True
 
-        def matmuls(dk, g):
-            first, n = GROUPS[g]
-            if g == 0:
+        def matmuls(dk):
+            if ("acc", dk) not in state:
                 state[("acc", dk)] = acc_pool.tile([P, NSEG * P], F32, name="acc")
             acc = state[("acc", dk)]
             wc, ws = state[("wc", dk)], state[("ws", dk)]
-            for s in range(2 * first, 2 * (first + n)):
+            s = state[("next_s", dk)]
+            if s == NS:
+                return
+            while s < NS and ("done", dk, s // 4) in state:
                 seg, f = divmod(s, KL)
                 w0 = SEG_WIN[seg]
                 nc.tensor.matmul_mx(
@@ -183,11 +235,13 @@ def tile_partiallyunsharedconv1d_pa_kernel(tc, x, weight_bytes, weight_scale, co
                     lhsT=wc[:, s * P:(s + 1) * P].bitcast(FP8X4),
                     lhsT_scale=ws[:, s * P:(s + 1) * P],
                     rhs=xc4[:, f, dk, w0:w0 + P].bitcast(FP8X4),
-                    rhs_scale=xs4[:, f, dk, w0:w0 + P],
+                    rhs_scale=xs4[:, f, dk, MARGIN + w0:MARGIN + w0 + P],
                     start=(f == 0),
                     stop=(f == KL - 1),
                 )
-            if g == len(GROUPS) - 1:
+                s += 1
+            state[("next_s", dk)] = s
+            if s == NS:
                 osb = out_pool.tile([P, L], F32, name="osb")
                 for seg in range(NSEG):
                     l0, ln = SEG_START[seg], SEG_LEN[seg]
@@ -198,29 +252,37 @@ def tile_partiallyunsharedconv1d_pa_kernel(tc, x, weight_bytes, weight_scale, co
                     )
                 nc.scalar.dma_start(out=out_rows[dk], in_=osb[:])
 
-        total = NDK * NBANK
+        total = len(banks)
         for b in range(LOOKAHEAD):
             transposes(b)
-        to_quantise = None
-        to_multiply = None
+        waiting = []
+        to_multiply = []
+        vjobs = 0
         for b in range(total):
-            dk, s2 = divmod(b, NBANK)
-            if s2 % 2 == 0 and s2 // 2 < NCH and dk + 1 < NDK:
-                c = s2 // 2
-                cast_w(dk + 1, c, on_vector=False)
+            dk, u, h = banks[b]
+            i = 2 * u + h
+            if i % 2 == 0 and i // 2 < NCH and dk + 1 < NDK:
+                cast_w(dk + 1, i // 2, on_vector=False)
                 if dk + 2 < NDK:
-                    load_w(dk + 2, c)
+                    load_w(dk + 2, i // 2)
             if b + LOOKAHEAD < total:
                 transposes(b + LOOKAHEAD)
-            closed = scale_bank(b)
-            if to_multiply is not None:
-                matmuls(*to_multiply)
-                to_multiply = None
-            if to_quantise is not None:
-                quantise(*to_quantise)
-                to_multiply = to_quantise
-            to_quantise = closed
-        if to_multiply is not None:
-            matmuls(*to_multiply)
-        quantise(*to_quantise)
-        matmuls(*to_quantise)
+            for g in to_multiply:
+                matmuls(g)
+            to_multiply = []
+            if consume(b):
+                vjobs += 1
+                for item in [w for w in waiting if w[0] <= vjobs]:
+                    quantise(item[1], item[2])
+                    waiting.remove(item)
+                    if item[1] not in to_multiply:
+                        to_multiply.append(item[1])
+                if h == 1:
+                    waiting.append([vjobs + 1, dk, u])
+            elif h == 1:
+                waiting.append([vjobs + SG_DUE[dk], dk, u])
+        for g in to_multiply:
+            matmuls(g)
+        for item in waiting:
+            quantise(item[1], item[2])
+            matmuls(item[1])

@@ -36,8 +36,9 @@ SEG_WIN = (0, 0, 64, 128)
 MARGIN = 64
 XROW = MARGIN + L
 LOOKAHEAD = 5
-SG_UNITS = ((8,), (8,), (6, 8), (0, 1, 3, 5, 7))
-SG_DUE = (5, 5, 5, 4)
+SG_UNITS = ((8,), (8,), (8,), (0, 2, 4, 6))
+SG_DUE = (9, 9, 7, 5)
+X_MOVES_AT = (3, 7, 11)
 HEAD_ON_VECTOR = (3, 4, 5)
 
 FLOPS = 2 * NDK * CO * CI * KL * L
@@ -49,7 +50,7 @@ def tile_partiallyunsharedconv1d_pa_kernel(tc, x, weight_bytes, weight_scale, co
         const = ctx.enter_context(tc.tile_pool(name="const", bufs=1))
         wb_pool = ctx.enter_context(tc.tile_pool(name="wb_pool", bufs=NCH))
         wbf_pool = ctx.enter_context(tc.tile_pool(name="wbf_pool", bufs=2))
-        grp_pool = ctx.enter_context(tc.tile_pool(name="grp_pool", bufs=5))
+        grp_pool = ctx.enter_context(tc.tile_pool(name="grp_pool", bufs=4))
         pl_pool = ctx.enter_context(tc.tile_pool(name="pl_pool", bufs=2))
         wq_pool = ctx.enter_context(tc.tile_pool(name="wq_pool", bufs=2))
         out_pool = ctx.enter_context(tc.tile_pool(name="out_pool", bufs=2))
@@ -81,7 +82,7 @@ def tile_partiallyunsharedconv1d_pa_kernel(tc, x, weight_bytes, weight_scale, co
         nc.vector.memset(zero[:], 0.0)
         warm = const.tile([P, 1], F32, name="warm")
         nc.scalar.activation(out=warm[:], in_=zero[:], func=IDENT, bias=zero[:, 0:1])
-        xraw = const.tile([P, NDK * 4 * L], BF16, name="xraw")
+        xraw = grp_pool.tile([P, 4096], BF16, name="grp", align_bytes=64)
         x_rows = x.rearrange("b d k (p t) l -> (b d k) p (t l)", t=4)
 
         def load_x(dk):
@@ -109,7 +110,7 @@ def tile_partiallyunsharedconv1d_pa_kernel(tc, x, weight_bytes, weight_scale, co
 
         xc = const.tile([P, KL * NDK * L], U32, name="xc", align_bytes=64)
         xs = const.tile([P, KL * NDK * XROW], U8, name="xs", align_bytes=64)
-        xg = const.tile([P, NDK * L * 4], BF16, name="xg", align_bytes=64)
+        xg = grp_pool.tile([P, 4096], BF16, name="grp", align_bytes=64)
         nc.vector.memset(xs[:].bitcast(I32), 0)
         xc_rows = xc[:].rearrange("p (g c) -> p g c", c=L)
         nc.vector.memset(xc_rows[:, :, 0:PAD].bitcast(I32), 0)
@@ -142,23 +143,32 @@ def tile_partiallyunsharedconv1d_pa_kernel(tc, x, weight_bytes, weight_scale, co
             nc.vector.tensor_copy(
                 out=xs4[:, PAD + sh, :, MARGIN - sh:XROW - sh], in_=xs4[:, PAD, :, MARGIN:XROW]
             )
-        for f in (0, 1, 2, 3):
-            nc.sync.dma_start(
-                out=xs4[:, f, :, MARGIN:XROW].bitcast(I32), in_=xs4[:, f + PAD, :, MARGIN - 4:XROW - 4].bitcast(I32)
-            )
-        nc.sync.dma_start(
-            out=xs4[:, 2 * PAD, :, MARGIN:XROW - 4].bitcast(I32), in_=xs4[:, PAD, :, MARGIN + 4:XROW].bitcast(I32)
-        )
-        for f in range(KL):
-            sh = f - PAD
-            if sh != 0:
-                lo, hi = max(0, -sh), L - max(0, sh)
+
+        def move_x_scales():
+            for f in (0, 1, 2, 3):
                 nc.sync.dma_start(
-                    out=xc4[:, f, :, lo:hi].bitcast(I32), in_=xc4[:, PAD, :, lo + sh:hi + sh].bitcast(I32)
+                    out=xs4[:, f, :, MARGIN:XROW].bitcast(I32),
+                    in_=xs4[:, f + PAD, :, MARGIN - 4:XROW - 4].bitcast(I32),
                 )
+            nc.sync.dma_start(
+                out=xs4[:, 2 * PAD, :, MARGIN:XROW - 4].bitcast(I32), in_=xs4[:, PAD, :, MARGIN + 4:XROW].bitcast(I32)
+            )
+
+        def move_x_codes(dk):
+            for f in range(KL):
+                sh = f - PAD
+                if sh != 0:
+                    lo, hi = max(0, -sh), L - max(0, sh)
+                    nc.sync.dma_start(
+                        out=xc4[:, f, dk, lo:hi].bitcast(I32), in_=xc4[:, PAD, dk, lo + sh:hi + sh].bitcast(I32)
+                    )
 
         for c in range(NCH):
             cast_w(0, c, on_vector=(c in HEAD_ON_VECTOR))
+        load_w(1, 0)
+        move_x_scales()
+        move_x_codes(0)
+        for c in range(1, NCH):
             load_w(1, c)
 
         banks = [(dk, u, h) for dk in range(NDK) for u in range(NUNIT) for h in range(2)]
@@ -178,12 +188,13 @@ def tile_partiallyunsharedconv1d_pa_kernel(tc, x, weight_bytes, weight_scale, co
         def consume(b):
             dk, u, h = banks[b]
             ps = state[("ps", b)]
-            if h == 0:
-                state[("grp", dk, u)] = grp_pool.tile([P, 2048], BF16, name="grp", align_bytes=64)
-            grp = state[("grp", dk, u)]
+            if ("grp", dk, u // 2) not in state:
+                state[("grp", dk, u // 2)] = grp_pool.tile([P, 4096], BF16, name="grp", align_bytes=64)
+            grp = state[("grp", dk, u // 2)]
+            base = (u % 2) * 2048
             if u not in SG_UNITS[dk]:
                 nc.vector.tensor_tensor(
-                    out=grp[:, h * 1024:(h + 1) * 1024].rearrange("p (e o t) -> p e o t", e=2, t=4),
+                    out=grp[:, base + h * 1024:base + (h + 1) * 1024].rearrange("p (e o t) -> p e o t", e=2, t=4),
                     in0=ps[:].bitcast(BF16).rearrange("p (t o e) -> p e o t", t=4, e=2),
                     in1=sc[:].to_broadcast([P, 2, P, 4]),
                     op=MULT,
@@ -202,7 +213,7 @@ def tile_partiallyunsharedconv1d_pa_kernel(tc, x, weight_bytes, weight_scale, co
                 rows = planes[:].rearrange("p (t j o e) -> p j e o t", t=4, j=2, e=2)
                 for j in range(2):
                     nc.gpsimd.tensor_scalar(
-                        out=grp[:, j * 1024:(j + 1) * 1024].rearrange("p (e o t) -> p e o t", e=2, t=4),
+                        out=grp[:, base + j * 1024:base + (j + 1) * 1024].rearrange("p (e o t) -> p e o t", e=2, t=4),
                         in0=rows[:, j], scalar1=1.0, scalar2=0.0, op0=MULT, op1=ADD,
                     )
             return False
@@ -212,12 +223,17 @@ def tile_partiallyunsharedconv1d_pa_kernel(tc, x, weight_bytes, weight_scale, co
                 state[("wc", dk)] = wq_pool.tile([P, NS * P], U32, name="wc", align_bytes=64)
                 state[("ws", dk)] = wq_pool.tile([P, NS * P], U8, name="ws", align_bytes=64)
                 state[("next_s", dk)] = 0
-            nc.vector.quantize_mx(
-                out=state[("wc", dk)][:, u * 512:(u + 1) * 512].bitcast(FP8X4),
-                scales=state[("ws", dk)][:, u * 512:(u + 1) * 512],
-                in_=state[("grp", dk, u)][:],
-            )
-            state[("done", dk, u)] = True
+            state[("ready", dk, u)] = True
+            pair = [v for v in (u - u % 2, u - u % 2 + 1) if v < NUNIT]
+            if all(("ready", dk, v) in state for v in pair):
+                a, w = pair[0] * 512, len(pair) * 512
+                nc.vector.quantize_mx(
+                    out=state[("wc", dk)][:, a:a + w].bitcast(FP8X4),
+                    scales=state[("ws", dk)][:, a:a + w],
+                    in_=state[("grp", dk, u // 2)][:, 0:4 * w],
+                )
+                for v in pair:
+                    state[("done", dk, v)] = True
 
         def matmuls(dk):
             if ("acc", dk) not in state:
@@ -265,6 +281,8 @@ def tile_partiallyunsharedconv1d_pa_kernel(tc, x, weight_bytes, weight_scale, co
                 cast_w(dk + 1, i // 2, on_vector=False)
                 if dk + 2 < NDK:
                     load_w(dk + 2, i // 2)
+            if b in X_MOVES_AT:
+                move_x_codes(X_MOVES_AT.index(b) + 1)
             if b + LOOKAHEAD < total:
                 transposes(b + LOOKAHEAD)
             for g in to_multiply:

@@ -35,9 +35,10 @@ SEG_LEN = (58, 58, 58, 82)
 SEG_WIN = (0, 0, 64, 128)
 MARGIN = 64
 XROW = MARGIN + L
-LOOKAHEAD = 5
+LOOKAHEAD = 6
+MIN_BATCH = 16
 SG_UNITS = ((8,), (8,), (8,), (0, 2, 4, 6))
-SG_DUE = (9, 9, 7, 5)
+SG_DUE = (9, 9, 7, 3)
 X_MOVES_AT = (3, 7, 11)
 HEAD_ON_VECTOR = (3, 4, 5)
 
@@ -48,14 +49,14 @@ def tile_partiallyunsharedconv1d_pa_kernel(tc, x, weight_bytes, weight_scale, co
     nc = tc.nc
     with ExitStack() as ctx:
         const = ctx.enter_context(tc.tile_pool(name="const", bufs=1))
-        wb_pool = ctx.enter_context(tc.tile_pool(name="wb_pool", bufs=NCH))
+        wb_pool = ctx.enter_context(tc.tile_pool(name="wb_pool", bufs=NCH + 2))
         wbf_pool = ctx.enter_context(tc.tile_pool(name="wbf_pool", bufs=2))
         grp_pool = ctx.enter_context(tc.tile_pool(name="grp_pool", bufs=4))
         pl_pool = ctx.enter_context(tc.tile_pool(name="pl_pool", bufs=2))
         wq_pool = ctx.enter_context(tc.tile_pool(name="wq_pool", bufs=2))
         out_pool = ctx.enter_context(tc.tile_pool(name="out_pool", bufs=2))
-        ps_pool = ctx.enter_context(tc.psum_pool(name="ps_pool", bufs=6))
-        acc_pool = ctx.enter_context(tc.psum_pool(name="acc_pool", bufs=2))
+        ps_pool = ctx.enter_context(tc.psum_pool(name="ps_pool", bufs=7))
+        acc_pool = ctx.enter_context(tc.psum_pool(name="acc_pool", bufs=1))
 
         w_rows = weight_bytes.rearrange("d k o i g u f -> (d k) o (i g u f)")
         out_rows = out.rearrange("b d k o l -> (b d k) o l")
@@ -94,6 +95,8 @@ def tile_partiallyunsharedconv1d_pa_kernel(tc, x, weight_bytes, weight_scale, co
             load_x(dk)
         for c in range(1, NCH):
             load_w(0, c)
+        load_w(1, 0)
+        load_w(1, 1)
 
         sc = const.tile([P, 1, 1, 4], F32, name="sc")
         nc.scalar.dma_start(
@@ -165,10 +168,9 @@ def tile_partiallyunsharedconv1d_pa_kernel(tc, x, weight_bytes, weight_scale, co
 
         for c in range(NCH):
             cast_w(0, c, on_vector=(c in HEAD_ON_VECTOR))
-        load_w(1, 0)
         move_x_scales()
         move_x_codes(0)
-        for c in range(1, NCH):
+        for c in range(2, NCH):
             load_w(1, c)
 
         banks = [(dk, u, h) for dk in range(NDK) for u in range(NUNIT) for h in range(2)]
@@ -236,13 +238,16 @@ def tile_partiallyunsharedconv1d_pa_kernel(tc, x, weight_bytes, weight_scale, co
                     state[("done", dk, v)] = True
 
         def matmuls(dk):
+            s = state[("next_s", dk)]
+            run = 0
+            while s + run < NS and ("done", dk, (s + run) // 4) in state:
+                run += 1
+            if run == 0 or (run < MIN_BATCH and s + run < NS):
+                return
             if ("acc", dk) not in state:
                 state[("acc", dk)] = acc_pool.tile([P, NSEG * P], F32, name="acc")
             acc = state[("acc", dk)]
             wc, ws = state[("wc", dk)], state[("ws", dk)]
-            s = state[("next_s", dk)]
-            if s == NS:
-                return
             while s < NS and ("done", dk, s // 4) in state:
                 seg, f = divmod(s, KL)
                 w0 = SEG_WIN[seg]

@@ -35,12 +35,11 @@ SEG_LEN = (58, 58, 58, 82)
 SEG_WIN = (0, 0, 64, 128)
 MARGIN = 64
 XROW = MARGIN + L
-LOOKAHEAD = 6
-MIN_BATCH = 16
+LOOKAHEAD = 5
 SG_UNITS = ((8,), (8,), (8,), (0, 2, 4, 6))
-SG_DUE = (9, 9, 7, 3)
+SG_DUE = (9, 9, 7, 5)
 X_MOVES_AT = (3, 7, 11)
-HEAD_ON_VECTOR = (3, 4, 5)
+HEAD_ON_VECTOR = (4, 5)
 
 FLOPS = 2 * NDK * CO * CI * KL * L
 
@@ -49,14 +48,14 @@ def tile_partiallyunsharedconv1d_pa_kernel(tc, x, weight_bytes, weight_scale, co
     nc = tc.nc
     with ExitStack() as ctx:
         const = ctx.enter_context(tc.tile_pool(name="const", bufs=1))
-        wb_pool = ctx.enter_context(tc.tile_pool(name="wb_pool", bufs=NCH + 2))
+        wb_pool = ctx.enter_context(tc.tile_pool(name="wb_pool", bufs=NCH))
         wbf_pool = ctx.enter_context(tc.tile_pool(name="wbf_pool", bufs=2))
         grp_pool = ctx.enter_context(tc.tile_pool(name="grp_pool", bufs=4))
         pl_pool = ctx.enter_context(tc.tile_pool(name="pl_pool", bufs=2))
         wq_pool = ctx.enter_context(tc.tile_pool(name="wq_pool", bufs=2))
         out_pool = ctx.enter_context(tc.tile_pool(name="out_pool", bufs=2))
-        ps_pool = ctx.enter_context(tc.psum_pool(name="ps_pool", bufs=7))
-        acc_pool = ctx.enter_context(tc.psum_pool(name="acc_pool", bufs=1))
+        ps_pool = ctx.enter_context(tc.psum_pool(name="ps_pool", bufs=6))
+        acc_pool = ctx.enter_context(tc.psum_pool(name="acc_pool", bufs=2))
 
         w_rows = weight_bytes.rearrange("d k o i g u f -> (d k) o (i g u f)")
         out_rows = out.rearrange("b d k o l -> (b d k) o l")
@@ -95,8 +94,6 @@ def tile_partiallyunsharedconv1d_pa_kernel(tc, x, weight_bytes, weight_scale, co
             load_x(dk)
         for c in range(1, NCH):
             load_w(0, c)
-        load_w(1, 0)
-        load_w(1, 1)
 
         sc = const.tile([P, 1, 1, 4], F32, name="sc")
         nc.scalar.dma_start(
@@ -168,9 +165,10 @@ def tile_partiallyunsharedconv1d_pa_kernel(tc, x, weight_bytes, weight_scale, co
 
         for c in range(NCH):
             cast_w(0, c, on_vector=(c in HEAD_ON_VECTOR))
+        load_w(1, 0)
         move_x_scales()
         move_x_codes(0)
-        for c in range(2, NCH):
+        for c in range(1, NCH):
             load_w(1, c)
 
         banks = [(dk, u, h) for dk in range(NDK) for u in range(NUNIT) for h in range(2)]
@@ -238,16 +236,13 @@ def tile_partiallyunsharedconv1d_pa_kernel(tc, x, weight_bytes, weight_scale, co
                     state[("done", dk, v)] = True
 
         def matmuls(dk):
-            s = state[("next_s", dk)]
-            run = 0
-            while s + run < NS and ("done", dk, (s + run) // 4) in state:
-                run += 1
-            if run == 0 or (run < MIN_BATCH and s + run < NS):
-                return
             if ("acc", dk) not in state:
                 state[("acc", dk)] = acc_pool.tile([P, NSEG * P], F32, name="acc")
             acc = state[("acc", dk)]
             wc, ws = state[("wc", dk)], state[("ws", dk)]
+            s = state[("next_s", dk)]
+            if s == NS:
+                return
             while s < NS and ("done", dk, s // 4) in state:
                 seg, f = divmod(s, KL)
                 w0 = SEG_WIN[seg]

@@ -36,8 +36,10 @@ SEG_WIN = (0, 0, 64, 128)
 MARGIN = 64
 XROW = MARGIN + L
 LOOKAHEAD = 5
-SG_UNITS = ((8,), (8,), (8,), (0, 2, 4, 6))
+SG_UNITS = ((), (), (), (0, 2, 4, 6))
 SG_DUE = (9, 9, 7, 5)
+PLANE_PAIRS = ((0, 1), (0, 1), (0, 1), ())
+BATCHED = (True, True, True, False)
 X_MOVES_AT = (3, 7, 11)
 HEAD_ON_VECTOR = (4, 5)
 
@@ -52,6 +54,7 @@ def tile_partiallyunsharedconv1d_pa_kernel(tc, x, weight_bytes, weight_scale, co
         wbf_pool = ctx.enter_context(tc.tile_pool(name="wbf_pool", bufs=2))
         grp_pool = ctx.enter_context(tc.tile_pool(name="grp_pool", bufs=4))
         pl_pool = ctx.enter_context(tc.tile_pool(name="pl_pool", bufs=2))
+        g8_pool = ctx.enter_context(tc.tile_pool(name="g8_pool", bufs=1))
         wq_pool = ctx.enter_context(tc.tile_pool(name="wq_pool", bufs=2))
         out_pool = ctx.enter_context(tc.tile_pool(name="out_pool", bufs=2))
         ps_pool = ctx.enter_context(tc.psum_pool(name="ps_pool", bufs=6))
@@ -178,7 +181,9 @@ def tile_partiallyunsharedconv1d_pa_kernel(tc, x, weight_bytes, weight_scale, co
             words = state[("wbf", dk)][:].bitcast(F32)
             ps = ps_pool.tile([P, 4 * P], F32, name="ps")
             for q in range(4):
-                if u in SG_UNITS[dk]:
+                if u // 2 in PLANE_PAIRS[dk]:
+                    t, s2 = 2 * (u % 2) + h, 4 * (u // 2) + q
+                elif u in SG_UNITS[dk]:
                     t, s2 = 2 * h + q // 2, 2 * u + q % 2
                 else:
                     t, s2 = q, 2 * u + h
@@ -189,9 +194,28 @@ def tile_partiallyunsharedconv1d_pa_kernel(tc, x, weight_bytes, weight_scale, co
             dk, u, h = banks[b]
             ps = state[("ps", b)]
             if ("grp", dk, u // 2) not in state:
-                state[("grp", dk, u // 2)] = grp_pool.tile([P, 4096], BF16, name="grp", align_bytes=64)
+                if u == NUNIT - 1:
+                    state[("grp", dk, u // 2)] = g8_pool.tile([P, 2048], BF16, name="grp8", align_bytes=64)
+                else:
+                    state[("grp", dk, u // 2)] = grp_pool.tile([P, 4096], BF16, name="grp", align_bytes=64)
             grp = state[("grp", dk, u // 2)]
             base = (u % 2) * 2048
+            if u // 2 in PLANE_PAIRS[dk]:
+                t = 2 * (u % 2) + h
+                if t == 0:
+                    state[("planes", dk, u // 2)] = pl_pool.tile([P, 4096], BF16, name="planes")
+                planes = state[("planes", dk, u // 2)]
+                nc.vector.tensor_scalar(
+                    out=planes[:, t * 1024:(t + 1) * 1024], in0=ps[:].bitcast(BF16),
+                    scalar1=sc[:, 0, 0, t:t + 1], scalar2=None, op0=MULT,
+                )
+                if t == 3:
+                    nc.gpsimd.tensor_scalar(
+                        out=grp[:].rearrange("p (e c t) -> p e c t", e=2, t=4),
+                        in0=planes[:].rearrange("p (t c e) -> p e c t", t=4, e=2),
+                        scalar1=1.0, scalar2=0.0, op0=MULT, op1=ADD,
+                    )
+                return True
             if u not in SG_UNITS[dk]:
                 nc.vector.tensor_tensor(
                     out=grp[:, base + h * 1024:base + (h + 1) * 1024].rearrange("p (e o t) -> p e o t", e=2, t=4),
@@ -246,10 +270,13 @@ def tile_partiallyunsharedconv1d_pa_kernel(tc, x, weight_bytes, weight_scale, co
             while s < NS and ("done", dk, s // 4) in state:
                 seg, f = divmod(s, KL)
                 w0 = SEG_WIN[seg]
+                col = s
+                if s // 8 in PLANE_PAIRS[dk]:
+                    col = 8 * (s // 8) + 4 * (s % 2) + (s % 8) // 2
                 nc.tensor.matmul_mx(
                     out=acc[:, seg * P:(seg + 1) * P],
-                    lhsT=wc[:, s * P:(s + 1) * P].bitcast(FP8X4),
-                    lhsT_scale=ws[:, s * P:(s + 1) * P],
+                    lhsT=wc[:, col * P:(col + 1) * P].bitcast(FP8X4),
+                    lhsT_scale=ws[:, col * P:(col + 1) * P],
                     rhs=xc4[:, f, dk, w0:w0 + P].bitcast(FP8X4),
                     rhs_scale=xs4[:, f, dk, MARGIN + w0:MARGIN + w0 + P],
                     start=(f == 0),
@@ -258,6 +285,16 @@ def tile_partiallyunsharedconv1d_pa_kernel(tc, x, weight_bytes, weight_scale, co
                 s += 1
             state[("next_s", dk)] = s
             if s == NS:
+                if BATCHED[dk]:
+                    to_store.append(dk)
+                else:
+                    store(dk)
+
+        to_store = []
+
+        def store(dk):
+            acc = state[("acc", dk)]
+            if True:
                 osb = out_pool.tile([P, L], F32, name="osb")
                 for seg in range(NSEG):
                     l0, ln = SEG_START[seg], SEG_LEN[seg]
@@ -281,6 +318,10 @@ def tile_partiallyunsharedconv1d_pa_kernel(tc, x, weight_bytes, weight_scale, co
                 cast_w(dk + 1, i // 2, on_vector=False)
                 if dk + 2 < NDK:
                     load_w(dk + 2, i // 2)
+            if i == 1:
+                for g in to_store:
+                    store(g)
+                to_store.clear()
             if b in X_MOVES_AT:
                 move_x_codes(X_MOVES_AT.index(b) + 1)
             if b + LOOKAHEAD < total:
@@ -288,7 +329,15 @@ def tile_partiallyunsharedconv1d_pa_kernel(tc, x, weight_bytes, weight_scale, co
             for g in to_multiply:
                 matmuls(g)
             to_multiply = []
-            if consume(b):
+            if BATCHED[dk]:
+                consume(b)
+                vjobs += 1
+                if i == NBANK - 1:
+                    for v in range(NUNIT):
+                        quantise(dk, v)
+                        if v % 2 == 1 or v == NUNIT - 1:
+                            matmuls(dk)
+            elif consume(b):
                 vjobs += 1
                 for item in [w for w in waiting if w[0] <= vjobs]:
                     quantise(item[1], item[2])

@@ -26,6 +26,7 @@ NS = NSEG * KL
 ROW = CI * NS
 CHUNK = 3072
 NCH = ROW // CHUNK
+FIRST = 1024
 NUNIT = NS // 4
 NBANK = 2 * NUNIT
 HALF = NS // 2
@@ -38,6 +39,7 @@ XROW = MARGIN + L
 LOOKAHEAD = 5
 SG_UNITS = ((), (), (), (0, 2, 4, 6))
 SG_DUE = (9, 9, 7, 5)
+SS_UNITS = ((), (), (), (7,))
 PLANE_PAIRS = ((0, 1), (0, 1), (0, 1), ())
 BATCHED = (True, True, True, False)
 X_MOVES_AT = (3, 7, 11)
@@ -91,8 +93,11 @@ def tile_partiallyunsharedconv1d_pa_kernel(tc, x, weight_bytes, weight_scale, co
         def load_x(dk):
             nc.sync.dma_start(out=xraw[:, dk * 4 * L:(dk + 1) * 4 * L], in_=x_rows[dk])
 
+        first = wb_pool.tile([P, CHUNK], U8, name="wbytes")
+        state[("wbytes", 0, 0)] = first
+        nc.sync.dma_start(out=first[:, 0:FIRST], in_=w_rows[0][:, 0:FIRST])
         load_x(0)
-        load_w(0, 0)
+        nc.sync.dma_start(out=first[:, FIRST:CHUNK], in_=w_rows[0][:, FIRST:CHUNK])
         for dk in range(1, NDK):
             load_x(dk)
         for c in range(1, NCH):
@@ -166,7 +171,10 @@ def tile_partiallyunsharedconv1d_pa_kernel(tc, x, weight_bytes, weight_scale, co
                         out=xc4[:, f, dk, lo:hi].bitcast(I32), in_=xc4[:, PAD, dk, lo + sh:hi + sh].bitcast(I32)
                     )
 
-        for c in range(NCH):
+        state[("wbf", 0)] = wbf_pool.tile([P, ROW], BF16, name="wbf")
+        nc.scalar.copy(out=state[("wbf", 0)][:, 0:FIRST], in_=first[:, 0:FIRST].bitcast(FP8))
+        nc.scalar.copy(out=state[("wbf", 0)][:, FIRST:CHUNK], in_=first[:, FIRST:CHUNK].bitcast(FP8))
+        for c in range(1, NCH):
             cast_w(0, c, on_vector=(c in HEAD_ON_VECTOR))
         load_w(1, 0)
         move_x_scales()
@@ -183,7 +191,7 @@ def tile_partiallyunsharedconv1d_pa_kernel(tc, x, weight_bytes, weight_scale, co
             for q in range(4):
                 if u // 2 in PLANE_PAIRS[dk]:
                     t, s2 = 2 * (u % 2) + h, 4 * (u // 2) + q
-                elif u in SG_UNITS[dk]:
+                elif u in SG_UNITS[dk] or u in SS_UNITS[dk]:
                     t, s2 = 2 * h + q // 2, 2 * u + q % 2
                 else:
                     t, s2 = q, 2 * u + h
@@ -216,7 +224,7 @@ def tile_partiallyunsharedconv1d_pa_kernel(tc, x, weight_bytes, weight_scale, co
                         scalar1=1.0, scalar2=0.0, op0=MULT, op1=ADD,
                     )
                 return True
-            if u not in SG_UNITS[dk]:
+            if u not in SG_UNITS[dk] and u not in SS_UNITS[dk]:
                 nc.vector.tensor_tensor(
                     out=grp[:, base + h * 1024:base + (h + 1) * 1024].rearrange("p (e o t) -> p e o t", e=2, t=4),
                     in0=ps[:].bitcast(BF16).rearrange("p (t o e) -> p e o t", t=4, e=2),
@@ -236,6 +244,12 @@ def tile_partiallyunsharedconv1d_pa_kernel(tc, x, weight_bytes, weight_scale, co
             if h == 1:
                 rows = planes[:].rearrange("p (t j o e) -> p j e o t", t=4, j=2, e=2)
                 for j in range(2):
+                    if u in SS_UNITS[dk]:
+                        nc.scalar.copy(
+                            out=grp[:, base + j * 1024:base + (j + 1) * 1024].rearrange("p (e o t) -> p e o t", e=2, t=4),
+                            in_=rows[:, j],
+                        )
+                        continue
                     nc.gpsimd.tensor_scalar(
                         out=grp[:, base + j * 1024:base + (j + 1) * 1024].rearrange("p (e o t) -> p e o t", e=2, t=4),
                         in0=rows[:, j], scalar1=1.0, scalar2=0.0, op0=MULT, op1=ADD,

@@ -44,6 +44,8 @@ PLANE_PAIRS = ((0, 1), (0, 1), (0, 1), ())
 BATCHED = (True, True, True, False)
 X_MOVES_AT = (3, 7, 11)
 HEAD_ON_VECTOR = (4, 5)
+LATE_MATMULS = (0, 1)
+MM_AT = 9
 
 FLOPS = 2 * NDK * CO * CI * KL * L
 
@@ -332,7 +334,7 @@ def tile_partiallyunsharedconv1d_pa_kernel(tc, x, weight_bytes, weight_scale, co
                 cast_w(dk + 1, i // 2, on_vector=False)
                 if dk + 2 < NDK:
                     load_w(dk + 2, i // 2)
-            if i == 1:
+            if i == 1 or i == MM_AT + 2:
                 for g in to_store:
                     store(g)
                 to_store.clear()
@@ -343,13 +345,15 @@ def tile_partiallyunsharedconv1d_pa_kernel(tc, x, weight_bytes, weight_scale, co
             for g in to_multiply:
                 matmuls(g)
             to_multiply = []
+            if i == MM_AT and dk - 1 in LATE_MATMULS:
+                matmuls(dk - 1)
             if BATCHED[dk]:
                 consume(b)
                 vjobs += 1
                 if i == NBANK - 1:
                     for v in range(NUNIT):
                         quantise(dk, v)
-                        if v % 2 == 1 or v == NUNIT - 1:
+                        if (v % 2 == 1 or v == NUNIT - 1) and dk not in LATE_MATMULS:
                             matmuls(dk)
             elif consume(b):
                 vjobs += 1

from contextlib import ExitStack

import concourse.mybir as mybir
from concourse.masks import make_identity

F32 = mybir.dt.float32
BF16 = mybir.dt.bfloat16
I32 = mybir.dt.int32
U32 = mybir.dt.uint32
U8 = mybir.dt.uint8
FP8 = mybir.dt.float8_e4m3fn
FP8X4 = mybir.dt.float8_e4m3fn_x4
MULT = mybir.AluOpType.mult
ADD = mybir.AluOpType.add
IDENT = mybir.ActivationFunctionType.Identity

P = 128
NDK = 4
CI = 512
CO = 128
L = 256
NSEG = 4
KL = 9
PAD = 4
NS = NSEG * KL
ROW = CI * NS
CHUNK = 3072
NCH = ROW // CHUNK
FIRST = 1024
NUNIT = NS // 4
NBANK = 2 * NUNIT
HALF = NS // 2
WSTEP = 4 * HALF
SEG_START = (0, 58, 116, 174)
SEG_LEN = (58, 58, 58, 82)
SEG_WIN = (0, 0, 64, 128)
MARGIN = 64
XROW = MARGIN + L
LOOKAHEAD = 5
SG_UNITS = ((), (), (), (0, 2, 4, 6))
SG_DUE = (9, 9, 7, 5)
SS_UNITS = ((), (), (), (7,))
PLANE_PAIRS = ((0, 1), (0, 1), (0, 1), ())
BATCHED = (True, True, True, False)
X_MOVES_AT = (3, 7, 11)
HEAD_ON_VECTOR = (4, 5)
LATE_MATMULS = (0, 1)
MM_AT = 9

FLOPS = 2 * NDK * CO * CI * KL * L


def tile_partiallyunsharedconv1d_pa_kernel(tc, x, weight_bytes, weight_scale, conv_bias_param, out):
    nc = tc.nc
    with ExitStack() as ctx:
        const = ctx.enter_context(tc.tile_pool(name="const", bufs=1))
        wb_pool = ctx.enter_context(tc.tile_pool(name="wb_pool", bufs=NCH))
        wbf_pool = ctx.enter_context(tc.tile_pool(name="wbf_pool", bufs=2))
        grp_pool = ctx.enter_context(tc.tile_pool(name="grp_pool", bufs=4))
        pl_pool = ctx.enter_context(tc.tile_pool(name="pl_pool", bufs=2))
        g8_pool = ctx.enter_context(tc.tile_pool(name="g8_pool", bufs=1))
        wq_pool = ctx.enter_context(tc.tile_pool(name="wq_pool", bufs=2))
        out_pool = ctx.enter_context(tc.tile_pool(name="out_pool", bufs=2))
        ps_pool = ctx.enter_context(tc.psum_pool(name="ps_pool", bufs=6))
        acc_pool = ctx.enter_context(tc.psum_pool(name="acc_pool", bufs=2))

        w_rows = weight_bytes.rearrange("d k o i g u f -> (d k) o (i g u f)")
        out_rows = out.rearrange("b d k o l -> (b d k) o l")

        state = {}

        def load_w(dk, c):
            wbytes = wb_pool.tile([P, CHUNK], U8, name="wbytes")
            nc.sync.dma_start(out=wbytes[:], in_=w_rows[dk][:, c * CHUNK:(c + 1) * CHUNK])
            state[("wbytes", dk, c)] = wbytes

        def cast_w(dk, c, on_vector):
            if ("wbf", dk) not in state:
                state[("wbf", dk)] = wbf_pool.tile([P, ROW], BF16, name="wbf")
            wbf = state[("wbf", dk)]
            src = state[("wbytes", dk, c)][:].bitcast(FP8)
            dst = wbf[:, c * CHUNK:(c + 1) * CHUNK]
            if on_vector:
                nc.vector.tensor_copy(out=dst, in_=src)
            else:
                nc.scalar.copy(out=dst, in_=src)

        zero = const.tile([P, 1], F32, name="zero")
        nc.vector.memset(zero[:], 0.0)
        warm = const.tile([P, 1], F32, name="warm")
        nc.scalar.activation(out=warm[:], in_=zero[:], func=IDENT, bias=zero[:, 0:1])
        xraw = grp_pool.tile([P, 4096], BF16, name="grp", align_bytes=64)
        x_rows = x.rearrange("b d k (p t) l -> (b d k) p (t l)", t=4)

        def load_x(dk):
            nc.sync.dma_start(out=xraw[:, dk * 4 * L:(dk + 1) * 4 * L], in_=x_rows[dk])

        first = wb_pool.tile([P, CHUNK], U8, name="wbytes")
        state[("wbytes", 0, 0)] = first
        nc.sync.dma_start(out=first[:, 0:FIRST], in_=w_rows[0][:, 0:FIRST])
        load_x(0)
        nc.sync.dma_start(out=first[:, FIRST:CHUNK], in_=w_rows[0][:, FIRST:CHUNK])
        for dk in range(1, NDK):
            load_x(dk)
        for c in range(1, NCH):
            load_w(0, c)

        sc = const.tile([P, 1, 1, 4], F32, name="sc")
        nc.scalar.dma_start(
            out=sc[:].rearrange("p a b t -> p (a b t)"),
            in_=weight_scale.rearrange("a b c i e f g -> (a b c i e f g)").rearrange("(p t) -> p t", t=4),
        )
        bias_bf = const.tile([P, NDK * NSEG], BF16, name="bias_bf")
        nc.scalar.dma_start(
            out=bias_bf[:].rearrange("p (a g) -> p a g", a=NDK),
            in_=conv_bias_param.rearrange("d k o g u -> o (d k) (g u)"),
        )
        ident = const.tile([P, P], F32, name="ident")
        make_identity(nc, ident[:])

        xc = const.tile([P, KL * NDK * L], U32, name="xc", align_bytes=64)
        xs = const.tile([P, KL * NDK * XROW], U8, name="xs", align_bytes=64)
        xg = grp_pool.tile([P, 4096], BF16, name="grp", align_bytes=64)
        nc.vector.memset(xs[:].bitcast(I32), 0)
        xc_rows = xc[:].rearrange("p (g c) -> p g c", c=L)
        nc.vector.memset(xc_rows[:, :, 0:PAD].bitcast(I32), 0)
        nc.vector.memset(xc_rows[:, :, L - PAD:L].bitcast(I32), 0)
        bias = const.tile([P, NDK * NSEG], F32, name="bias")

        xc4 = xc[:].rearrange("p (f d c) -> p f d c", f=KL, d=NDK)
        xs4 = xs[:].rearrange("p (f d c) -> p f d c", f=KL, d=NDK)

        def interleave_x(dk):
            cols = slice(dk * 4 * L, (dk + 1) * 4 * L)
            nc.vector.tensor_copy(
                out=xg[:, cols].rearrange("p (l t) -> p l t", t=4), in_=xraw[:, cols].rearrange("p (t l) -> p l t", t=4)
            )

        def quantise_x(dk):
            nc.vector.quantize_mx(
                out=xc4[:, PAD, dk, :].bitcast(FP8X4),
                scales=xs4[:, PAD, dk, MARGIN:XROW],
                in_=xg[:, dk * 4 * L:(dk + 1) * 4 * L],
            )

        interleave_x(0)
        for dk in range(1, NDK):
            interleave_x(dk)
            quantise_x(dk - 1)
        nc.vector.tensor_copy(out=bias[:], in_=bias_bf[:])
        quantise_x(NDK - 1)
        for sh in (1, 2, 3):
            nc.vector.tensor_copy(
                out=xs4[:, PAD + sh, :, MARGIN - sh:XROW - sh], in_=xs4[:, PAD, :, MARGIN:XROW]
            )

        def move_x_scales():
            for f in (0, 1, 2, 3):
                nc.sync.dma_start(
                    out=xs4[:, f, :, MARGIN:XROW].bitcast(I32),
                    in_=xs4[:, f + PAD, :, MARGIN - 4:XROW - 4].bitcast(I32),
                )
            nc.sync.dma_start(
                out=xs4[:, 2 * PAD, :, MARGIN:XROW - 4].bitcast(I32), in_=xs4[:, PAD, :, MARGIN + 4:XROW].bitcast(I32)
            )

        def move_x_codes(dk):
            for f in range(KL):
                sh = f - PAD
                if sh != 0:
                    lo, hi = max(0, -sh), L - max(0, sh)
                    nc.sync.dma_start(
                        out=xc4[:, f, dk, lo:hi].bitcast(I32), in_=xc4[:, PAD, dk, lo + sh:hi + sh].bitcast(I32)
                    )

        state[("wbf", 0)] = wbf_pool.tile([P, ROW], BF16, name="wbf")
        nc.scalar.copy(out=state[("wbf", 0)][:, 0:FIRST], in_=first[:, 0:FIRST].bitcast(FP8))
        nc.scalar.copy(out=state[("wbf", 0)][:, FIRST:CHUNK], in_=first[:, FIRST:CHUNK].bitcast(FP8))
        for c in range(1, NCH):
            cast_w(0, c, on_vector=(c in HEAD_ON_VECTOR))
        load_w(1, 0)
        move_x_scales()
        move_x_codes(0)
        for c in range(1, NCH):
            load_w(1, c)

        banks = [(dk, u, h) for dk in range(NDK) for u in range(NUNIT) for h in range(2)]

        def transposes(b):
            dk, u, h = banks[b]
            words = state[("wbf", dk)][:].bitcast(F32)
            ps = ps_pool.tile([P, 4 * P], F32, name="ps")
            for q in range(4):
                if u // 2 in PLANE_PAIRS[dk]:
                    t, s2 = 2 * (u % 2) + h, 4 * (u // 2) + q
                elif u in SG_UNITS[dk] or u in SS_UNITS[dk]:
                    t, s2 = 2 * h + q // 2, 2 * u + q % 2
                else:
                    t, s2 = q, 2 * u + h
                nc.tensor.transpose(ps[:, q * P:(q + 1) * P], words[:, t * HALF + s2:ROW // 2:WSTEP], ident[:])
            state[("ps", b)] = ps

        def consume(b):
            dk, u, h = banks[b]
            ps = state[("ps", b)]
            if ("grp", dk, u // 2) not in state:
                if u == NUNIT - 1:
                    state[("grp", dk, u // 2)] = g8_pool.tile([P, 2048], BF16, name="grp8", align_bytes=64)
                else:
                    state[("grp", dk, u // 2)] = grp_pool.tile([P, 4096], BF16, name="grp", align_bytes=64)
            grp = state[("grp", dk, u // 2)]
            base = (u % 2) * 2048
            if u // 2 in PLANE_PAIRS[dk]:
                t = 2 * (u % 2) + h
                if t == 0:
                    state[("planes", dk, u // 2)] = pl_pool.tile([P, 4096], BF16, name="planes")
                planes = state[("planes", dk, u // 2)]
                nc.vector.tensor_scalar(
                    out=planes[:, t * 1024:(t + 1) * 1024], in0=ps[:].bitcast(BF16),
                    scalar1=sc[:, 0, 0, t:t + 1], scalar2=None, op0=MULT,
                )
                if t == 3:
                    nc.gpsimd.tensor_scalar(
                        out=grp[:].rearrange("p (e c t) -> p e c t", e=2, t=4),
                        in0=planes[:].rearrange("p (t c e) -> p e c t", t=4, e=2),
                        scalar1=1.0, scalar2=0.0, op0=MULT, op1=ADD,
                    )
                return True
            if u not in SG_UNITS[dk] and u not in SS_UNITS[dk]:
                nc.vector.tensor_tensor(
                    out=grp[:, base + h * 1024:base + (h + 1) * 1024].rearrange("p (e o t) -> p e o t", e=2, t=4),
                    in0=ps[:].bitcast(BF16).rearrange("p (t o e) -> p e o t", t=4, e=2),
                    in1=sc[:].to_broadcast([P, 2, P, 4]),
                    op=MULT,
                )
                return True
            if h == 0:
                state[("planes", dk, u)] = pl_pool.tile([P, 2048], BF16, name="planes")
            planes = state[("planes", dk, u)]
            for q in range(2):
                t = 2 * h + q
                nc.scalar.activation(
                    out=planes[:, t * 512:(t + 1) * 512], in_=ps[:, q * 256:(q + 1) * 256].bitcast(BF16),
                    func=IDENT, scale=sc[:, 0, 0, t:t + 1],
                )
            if h == 1:
                rows = planes[:].rearrange("p (t j o e) -> p j e o t", t=4, j=2, e=2)
                for j in range(2):
                    if u in SS_UNITS[dk]:
                        nc.scalar.copy(
                            out=grp[:, base + j * 1024:base + (j + 1) * 1024].rearrange("p (e o t) -> p e o t", e=2, t=4),
                            in_=rows[:, j],
                        )
                        continue
                    nc.gpsimd.tensor_scalar(
                        out=grp[:, base + j * 1024:base + (j + 1) * 1024].rearrange("p (e o t) -> p e o t", e=2, t=4),
                        in0=rows[:, j], scalar1=1.0, scalar2=0.0, op0=MULT, op1=ADD,
                    )
            return False

        def quantise(dk, u):
            if ("wc", dk) not in state:
                state[("wc", dk)] = wq_pool.tile([P, NS * P], U32, name="wc", align_bytes=64)
                state[("ws", dk)] = wq_pool.tile([P, NS * P], U8, name="ws", align_bytes=64)
                state[("next_s", dk)] = 0
            state[("ready", dk, u)] = True
            pair = [v for v in (u - u % 2, u - u % 2 + 1) if v < NUNIT]
            if all(("ready", dk, v) in state for v in pair):
                a, w = pair[0] * 512, len(pair) * 512
                nc.vector.quantize_mx(
                    out=state[("wc", dk)][:, a:a + w].bitcast(FP8X4),
                    scales=state[("ws", dk)][:, a:a + w],
                    in_=state[("grp", dk, u // 2)][:, 0:4 * w],
                )
                for v in pair:
                    state[("done", dk, v)] = True

        def matmuls(dk):
            if ("acc", dk) not in state:
                state[("acc", dk)] = acc_pool.tile([P, NSEG * P], F32, name="acc")
            acc = state[("acc", dk)]
            wc, ws = state[("wc", dk)], state[("ws", dk)]
            s = state[("next_s", dk)]
            if s == NS:
                return
            while s < NS and ("done", dk, s // 4) in state:
                seg, f = divmod(s, KL)
                w0 = SEG_WIN[seg]
                col = s
                if s // 8 in PLANE_PAIRS[dk]:
                    col = 8 * (s // 8) + 4 * (s % 2) + (s % 8) // 2
                nc.tensor.matmul_mx(
                    out=acc[:, seg * P:(seg + 1) * P],
                    lhsT=wc[:, col * P:(col + 1) * P].bitcast(FP8X4),
                    lhsT_scale=ws[:, col * P:(col + 1) * P],
                    rhs=xc4[:, f, dk, w0:w0 + P].bitcast(FP8X4),
                    rhs_scale=xs4[:, f, dk, MARGIN + w0:MARGIN + w0 + P],
                    start=(f == 0),
                    stop=(f == KL - 1),
                )
                s += 1
            state[("next_s", dk)] = s
            if s == NS:
                if BATCHED[dk]:
                    to_store.append(dk)
                else:
                    store(dk)

        to_store = []

        def store(dk):
            acc = state[("acc", dk)]
            if True:
                osb = out_pool.tile([P, L], F32, name="osb")
                for seg in range(NSEG):
                    l0, ln = SEG_START[seg], SEG_LEN[seg]
                    a0 = seg * P + l0 - SEG_WIN[seg]
                    nc.scalar.activation(
                        out=osb[:, l0:l0 + ln], in_=acc[:, a0:a0 + ln], func=IDENT,
                        bias=bias[:, dk * NSEG + seg:dk * NSEG + seg + 1],
                    )
                nc.scalar.dma_start(out=out_rows[dk], in_=osb[:])

        total = len(banks)
        for b in range(LOOKAHEAD):
            transposes(b)
        waiting = []
        to_multiply = []
        vjobs = 0
        for b in range(total):
            dk, u, h = banks[b]
            i = 2 * u + h
            if i % 2 == 0 and i // 2 < NCH and dk + 1 < NDK:
                cast_w(dk + 1, i // 2, on_vector=False)
                if dk + 2 < NDK:
                    load_w(dk + 2, i // 2)
            if i == 1 or i == MM_AT + 2:
                for g in to_store:
                    store(g)
                to_store.clear()
            if b in X_MOVES_AT:
                move_x_codes(X_MOVES_AT.index(b) + 1)
            if b + LOOKAHEAD < total:
                transposes(b + LOOKAHEAD)
            for g in to_multiply:
                matmuls(g)
            to_multiply = []
            if i == MM_AT and dk - 1 in LATE_MATMULS:
                matmuls(dk - 1)
            if BATCHED[dk]:
                consume(b)
                vjobs += 1
                if i == NBANK - 1:
                    for v in range(NUNIT):
                        quantise(dk, v)
                        if (v % 2 == 1 or v == NUNIT - 1) and dk not in LATE_MATMULS:
                            matmuls(dk)
            elif consume(b):
                vjobs += 1
                for item in [w for w in waiting if w[0] <= vjobs]:
                    quantise(item[1], item[2])
                    waiting.remove(item)
                    if item[1] not in to_multiply:
                        to_multiply.append(item[1])
                if h == 1:
                    waiting.append([vjobs + 1, dk, u])
            elif h == 1:
                waiting.append([vjobs + SG_DUE[dk], dk, u])
        for g in to_multiply:
            matmuls(g)
        for item in waiting:
            quantise(item[1], item[2])
            matmuls(item[1])
